import numpy as np
import ml_dtypes


def mxq(x, axis, fmt="e4m3"):
    dtype, down = {"e4m3": (ml_dtypes.float8_e4m3fn, 7), "e5m2": (ml_dtypes.float8_e5m2, 14)}[fmt]
    v = np.moveaxis(np.asarray(x, np.float32).astype(ml_dtypes.bfloat16).astype(np.float64), axis, -1)
    blocks = v.reshape(v.shape[:-1] + (-1, 32))
    amax = np.abs(blocks).max(-1, keepdims=True)
    byte = np.maximum(np.where(amax > 0, np.frexp(amax)[1] - 1 + 127, 0) - down, 1)
    scale = np.exp2(byte - 127.0)
    codes = (blocks / scale).astype(np.float32).astype(dtype).astype(np.float64)
    return np.moveaxis((codes * scale).reshape(v.shape), -1, axis)


WIDE = False


def mx_kscale(k):
    if not WIDE:
        return np.ones(k)
    levels = np.array([10, -10, 5, -5, 0])
    if k % 512:
        return np.exp2(np.random.permutation(np.resize(levels, k // 32))).repeat(32)
    a = np.empty((k // 512, 16))
    for p in range(k // 512):
        a[p, :8] = np.random.permutation(np.resize(levels, 8))
        for g in range(8):
            far = levels[np.abs(levels - a[p, g]) >= 10]
            a[p, g + 8] = far[np.random.randint(len(far))]
    return np.exp2(a.ravel()).repeat(32)


BF16 = ml_dtypes.bfloat16


def bf(x):
    return np.asarray(x, np.float32).astype(BF16)


def f64(x):
    return np.asarray(x).astype(np.float64)


B, F, C, H = 2, 256, 7936, 256
K = C + H


def sigmoid(v):
    return 1.0 / (1.0 + np.exp(-v))


def setup_inputs():
    s = mx_kscale(K)

    def w():
        return bf(np.random.standard_normal((H, K)) / np.sqrt(K) / s[None, :])

    def b():
        return bf(np.random.standard_normal(H) * 0.3)

    return {"x": bf(np.random.standard_normal((B, F, C)) * s[None, None, :C]),
            "hidden_state": bf(np.random.standard_normal((B, H, F)) * s[None, C:, None]),
            "cell_state": bf(np.random.standard_normal((B, H, F))),
            "W_f": w(), "b_f": b(), "W_i": w(), "b_i": b(), "W_o": w(), "b_o": b(), "W_g": w(), "b_g": b()}


def reference(x, hidden_state, cell_state, W_f, b_f, W_i, b_i, W_o, b_o, W_g, b_g):
    xh = np.concatenate([np.swapaxes(f64(x), 1, 2), f64(hidden_state)], axis=1)
    W = np.concatenate([f64(W_f), f64(W_i), f64(W_g), f64(W_o)], axis=0)
    b = np.concatenate([f64(b_f), f64(b_i), f64(b_g), f64(b_o)], axis=0)
    gates = (mxq(W, 1, "e4m3") @ mxq(xh, 1, "e4m3")) + b[None, :, None]
    f_t = sigmoid(gates[:, 0 * H:1 * H])
    i_t = sigmoid(gates[:, 1 * H:2 * H])
    g_t = np.tanh(gates[:, 2 * H:3 * H])
    o_t = sigmoid(gates[:, 3 * H:4 * H])
    new_cell = f64(cell_state) * f_t + i_t * g_t
    new_hidden = np.tanh(new_cell) * o_t
    return (np.swapaxes(new_hidden, 1, 2), new_hidden, new_cell)

@@ -1,0 +1,340 @@
+from contextlib import ExitStack
+
+import concourse.mybir as mybir
+from concourse.masks import make_identity
+
+F32 = mybir.dt.float32
+BF16 = mybir.dt.bfloat16
+U32 = mybir.dt.uint32
+U8 = mybir.dt.uint8
+FP8X4 = mybir.dt.float8_e4m3fn_x4
+ACT = mybir.ActivationFunctionType
+ALU = mybir.AluOpType
+
+P = 128
+HALF = P // 2
+PACK = 4
+K_PASS = P * PACK
+PASS_WORDS = K_PASS // 2
+BANK_WORDS = 512
+
+BATCH, FRAMES, CHANNELS, HIDDEN = 2, 256, 7936, 256
+K = CHANNELS + HIDDEN
+PASSES = K // K_PASS
+N = BATCH * FRAMES
+ROW_TILES = N // P
+GATES = 4
+H_TILES = HIDDEN // P
+
+CHUNK_PASSES = 2
+CHUNK_K = CHUNK_PASSES * K_PASS
+CHUNKS = K // CHUNK_K
+LOAD_AHEAD = 3
+
+FREE_BANKS = 4
+OPERAND_BANKS = 2
+BANK_TILES = 2
+BANK_COLUMNS = BANK_TILES * P
+
+IDLE_MATMULS = 3
+FLIP_LAG = 5
+
+FLOPS = 2 * GATES * HIDDEN * K * N
+
+
+def tile_batchedlstm_k_kernel(
+    tc, x, hidden_state, cell_state, W_f, b_f, W_i, b_i, W_o, b_o, W_g, b_g, out_0, out_1, out_2
+):
+    nc = tc.nc
+    weights = (W_f, W_i, W_g, W_o)
+    biases = (b_f, b_i, b_g, b_o)
+    gate_functions = (ACT.Sigmoid, ACT.Sigmoid, ACT.Tanh, ACT.Sigmoid)
+    x_rows = x.rearrange("b f c -> (b f) c")
+
+    rounds = []
+    for h_tile, operands_a_pass in ((0, 2), (1, 1)):
+        round_passes = FREE_BANKS // (OPERAND_BANKS * operands_a_pass)
+        rounds += [(h_tile, list(range(g, g + round_passes))) for g in range(0, PASSES, round_passes)]
+
+    with ExitStack() as ctx:
+        ctx.enter_context(tc.manual_schedule())
+        keep = ctx.enter_context(tc.tile_pool(name="keep", bufs=1))
+        x_raw_pool = ctx.enter_context(tc.tile_pool(name="x_raw", bufs=ROW_TILES * (LOAD_AHEAD + 1)))
+        w_raw_pool = ctx.enter_context(tc.tile_pool(name="w_raw", bufs=GATES * (LOAD_AHEAD + 1)))
+        grouped_pool = ctx.enter_context(tc.tile_pool(name="grouped", bufs=2 * FREE_BANKS))
+        w_mx_pool = ctx.enter_context(tc.tile_pool(name="w_mx", bufs=4))
+        cell_pool = ctx.enter_context(tc.tile_pool(name="cell", bufs=H_TILES * BATCH))
+        acc_pool = ctx.enter_context(tc.psum_pool(name="acc", bufs=1))
+        bank_pool = ctx.enter_context(tc.psum_pool(name="bank", bufs=FREE_BANKS))
+
+        identity = keep.tile([P, P], F32, name="identity")
+        make_identity(nc, identity[:])
+        zeros = keep.tile([P, N], BF16, name="zeros")
+        nc.vector.memset(zeros[:], 0.0)
+
+        bias_rows = keep.tile([P, P], BF16, name="bias_rows")
+        nc.vector.memset(bias_rows[:], 0.0)
+        for gate in range(GATES):
+            nc.scalar.dma_start(
+                out=bias_rows[gate * H_TILES : (gate + 1) * H_TILES, :],
+                in_=biases[gate].rearrange("(t p) -> t p", p=P),
+            )
+        bias_columns = keep.tile([P, GATES * H_TILES], F32, name="bias_columns")
+
+        hidden_raw = keep.tile([P, BATCH, PACK * FRAMES], BF16, name="hidden_raw")
+        nc.scalar.dma_start(
+            out=hidden_raw[HALF:, :, :],
+            in_=hidden_state.rearrange("b (p t) f -> p b (t f)", t=PACK),
+        )
+        last_xh = keep.tile([P, N * PACK], BF16, align_bytes=64, name="last_xh")
+
+        warm = keep.tile([P, 1], F32, name="warm")
+        nc.vector.memset(warm[:], 0.0)
+        nc.scalar.activation(out=warm[:], in_=warm[:], func=ACT.Sigmoid)
+
+        def prepare_small_inputs():
+            bias_rows_f32 = keep.tile([P, P], F32, name="bias_rows_f32")
+            nc.vector.tensor_copy(out=bias_rows_f32[:], in_=bias_rows[:])
+            bank = bank_pool.tile([P, BANK_WORDS], F32, name="bank")
+            nc.tensor.transpose(bank[:, :P], bias_rows_f32[:], identity[:])
+            nc.vector.tensor_copy(out=bias_columns[:], in_=bank[:, : GATES * H_TILES])
+            nc.vector.tensor_copy(
+                out=last_xh[HALF:, :].rearrange("p (b f t) -> p b f t", b=BATCH, t=PACK),
+                in_=hidden_raw[HALF:, :, :].rearrange("p b (t f) -> p b f t", t=PACK),
+            )
+
+        idle_bank = acc_pool.tile([P, N], F32, name="acc0")
+
+        def hold_clock():
+            for repeat in range(IDLE_MATMULS):
+                nc.tensor.matmul(idle_bank[:], lhsT=zeros[:, :P], rhs=zeros[:], start=True, stop=True)
+
+        x_raw = {}
+        w_raw = {}
+        cell_raw = {}
+
+        def load_chunk(step):
+            h_tile, chunk = divmod(step, CHUNKS)
+            h_rows = slice(h_tile * P, (h_tile + 1) * P)
+            k0 = chunk * CHUNK_K
+            if h_tile == 0:
+                width = min(CHUNK_K, CHANNELS - k0)
+                for r in range(ROW_TILES):
+                    raw = x_raw_pool.tile([P, CHUNK_K], BF16, name="x_raw")
+                    if width < CHUNK_K:
+                        nc.gpsimd.memset(raw[:, width:], 0.0)
+                    nc.sync.dma_start(
+                        out=raw[:, :width], in_=x_rows[r * P : (r + 1) * P, k0 : k0 + width]
+                    )
+                    x_raw[(chunk, r)] = raw
+            for gate in range(GATES):
+                raw = w_raw_pool.tile([P, CHUNK_K], BF16, name="w_raw")
+                nc.sync.dma_start(out=raw[:], in_=weights[gate][h_rows, k0 : k0 + CHUNK_K])
+                w_raw[(h_tile, chunk, gate)] = raw
+            if chunk == CHUNKS - 1:
+                raw = cell_pool.tile([P, BATCH, FRAMES], BF16, name="cell_raw")
+                nc.sync.dma_start(out=raw[:], in_=cell_state.rearrange("b h f -> h b f")[h_rows])
+                cell_raw[h_tile] = raw
+
+        staged = {}
+
+        def transpose_operand(index, sources, first_word, codes, scales, vector_helps):
+            for half in range(OPERAND_BANKS):
+                bank = bank_pool.tile([P, BANK_WORDS], F32, name="bank")
+                planes = bank[:].rearrange("p (s u n) -> p s u n", s=BANK_TILES, u=2)
+                for s in range(BANK_TILES):
+                    words = sources[BANK_TILES * half + s][:].bitcast(F32)
+                    for u in range(2):
+                        w0 = first_word + u
+                        nc.tensor.transpose(
+                            planes[:, s, u, :], words[:, w0 : first_word + PASS_WORDS : 2], identity[:]
+                        )
+                grouped = grouped_pool.tile(
+                    [P, BANK_COLUMNS * PACK], BF16, align_bytes=64, name="grouped"
+                )
+                copy_out = nc.vector.tensor_copy if vector_helps and half == 1 else nc.scalar.copy
+                copy_out(
+                    out=grouped[:].bitcast(F32).rearrange("p (s n u) -> p s n u", s=BANK_TILES, u=2),
+                    in_=planes.rearrange("p s u n -> p s n u"),
+                )
+                columns = slice(half * BANK_COLUMNS, (half + 1) * BANK_COLUMNS)
+                staged[index].append((grouped[:], codes[:, columns], scales[:, columns]))
+
+        def transpose_last_xh(index, sources, first_word, codes, scales):
+            for half in range(OPERAND_BANKS):
+                bank = bank_pool.tile([P, BANK_WORDS], F32, name="bank")
+                planes = bank[:].rearrange("p (s u n) -> p s u n", s=BANK_TILES, u=2)
+                for s in range(BANK_TILES):
+                    words = sources[BANK_TILES * half + s][:].bitcast(F32)
+                    for u in range(2):
+                        w0 = first_word + u
+                        nc.tensor.transpose(
+                            planes[:, s, u, :], words[:, w0 : first_word + PASS_WORDS : 2], identity[:]
+                        )
+                columns = slice(half * BANK_COLUMNS * PACK, (half + 1) * BANK_COLUMNS * PACK)
+                copy_out = nc.vector.tensor_copy if half == 1 else nc.scalar.copy
+                copy_out(
+                    out=last_xh[:HALF, columns]
+                    .bitcast(F32)
+                    .rearrange("p (s n u) -> p s n u", s=BANK_TILES, u=2),
+                    in_=planes[:HALF].rearrange("p s u n -> p s n u"),
+                )
+            staged[index].append((last_xh[:], codes[:], scales[:]))
+
+        x_codes = {}
+        x_scales = {}
+        w_codes = {}
+        w_scales = {}
+
+        def stage(index):
+            h_tile, passes = rounds[index]
+            staged[index] = []
+            for g in passes:
+                chunk, pass_in_chunk = divmod(g, CHUNK_PASSES)
+                first_word = pass_in_chunk * PASS_WORDS
+                if h_tile == 0:
+                    sources = [x_raw[(chunk, r)] for r in range(ROW_TILES)]
+                    x_codes[g] = keep.tile([P, N], U32, align_bytes=64, name="x_codes%d" % g)
+                    x_scales[g] = keep.tile([P, N], U8, align_bytes=64, name="x_scales%d" % g)
+                    if g < PASSES - 1:
+                        transpose_operand(index, sources, first_word, x_codes[g], x_scales[g], True)
+                    else:
+                        transpose_last_xh(index, sources, first_word, x_codes[g], x_scales[g])
+                    if index == 0:
+                        hold_clock()
+                step = h_tile * CHUNKS + chunk
+                if pass_in_chunk == 0 and step + LOAD_AHEAD < H_TILES * CHUNKS:
+                    load_chunk(step + LOAD_AHEAD)
+                sources = [w_raw[(h_tile, chunk, gate)] for gate in range(GATES)]
+                codes = w_mx_pool.tile([P, GATES * P], U32, align_bytes=64, name="w_codes")
+                scales = w_mx_pool.tile([P, GATES * P], U8, align_bytes=64, name="w_scales")
+                w_codes[(h_tile, g)] = codes
+                w_scales[(h_tile, g)] = scales
+                first_operand = len(staged[index]) == 0
+                transpose_operand(index, sources, first_word, codes, scales, first_operand)
+                if index == 0:
+                    hold_clock()
+
+        def quantise(index):
+            for grouped, codes, scales in staged[index]:
+                nc.vector.quantize_mx(out=codes.bitcast(FP8X4), scales=scales, in_=grouped)
+
+        acc = {}
+
+        def multiply(index):
+            h_tile, passes = rounds[index]
+            for gate in range(GATES):
+                if passes[0] == 0:
+                    acc[(h_tile, gate)] = acc_pool.tile([P, N], F32, name="acc%d" % gate)
+                gate_columns = slice(gate * P, (gate + 1) * P)
+                for g in passes:
+                    nc.tensor.matmul_mx(
+                        out=acc[(h_tile, gate)][:],
+                        lhsT=w_codes[(h_tile, g)][:, gate_columns].bitcast(FP8X4),
+                        lhsT_scale=w_scales[(h_tile, g)][:, gate_columns],
+                        rhs=x_codes[g][:].bitcast(FP8X4),
+                        rhs_scale=x_scales[g][:],
+                        start=(g == 0),
+                        stop=(g == PASSES - 1),
+                    )
+
+        activated = {}
+        new_cell = {}
+        new_hidden = {}
+
+        def cell_tile(name):
+            return cell_pool.tile([P, FRAMES], F32, name=name)
+
+        def activate_gates(h_tile):
+            for gate in range(GATES):
+                bias_column = gate * H_TILES + h_tile
+                for b in range(BATCH):
+                    activated[(h_tile, gate, b)] = cell_tile("gate%d" % gate)
+                    nc.scalar.activation(
+                        out=activated[(h_tile, gate, b)][:],
+                        in_=acc[(h_tile, gate)][:, b * FRAMES : (b + 1) * FRAMES],
+                        func=gate_functions[gate],
+                        bias=bias_columns[:, bias_column : bias_column + 1],
+                        scale=1.0,
+                    )
+
+        def update_cell(h_tile):
+            h_rows = slice(h_tile * P, (h_tile + 1) * P)
+            kept = {}
+            for b in range(BATCH):
+                kept[b] = cell_tile("kept")
+                nc.vector.tensor_tensor(
+                    out=kept[b][:],
+                    in0=activated[(h_tile, 0, b)][:],
+                    in1=cell_raw[h_tile][:, b, :],
+                    op=ALU.mult,
+                )
+            for b in range(BATCH):
+                added = cell_tile("added")
+                nc.vector.tensor_tensor(
+                    out=added[:],
+                    in0=activated[(h_tile, 1, b)][:],
+                    in1=activated[(h_tile, 2, b)][:],
+                    op=ALU.mult,
+                )
+                new_cell[(h_tile, b)] = cell_tile("new_cell")
+                nc.vector.tensor_tensor(
+                    out=new_cell[(h_tile, b)][:], in0=kept[b][:], in1=added[:], op=ALU.add
+                )
+                nc.sync.dma_start(out=out_2[b, h_rows, :], in_=new_cell[(h_tile, b)][:])
+
+        def update_hidden(h_tile):
+            h_rows = slice(h_tile * P, (h_tile + 1) * P)
+            squashed = {}
+            for b in range(BATCH):
+                squashed[b] = cell_tile("squashed")
+                nc.scalar.activation(out=squashed[b][:], in_=new_cell[(h_tile, b)][:], func=ACT.Tanh)
+            for b in range(BATCH):
+                new_hidden[(h_tile, b)] = cell_tile("new_hidden")
+                nc.vector.tensor_tensor(
+                    out=new_hidden[(h_tile, b)][:],
+                    in0=squashed[b][:],
+                    in1=activated[(h_tile, 3, b)][:],
+                    op=ALU.mult,
+                )
+                nc.sync.dma_start(out=out_1[b, h_rows, :], in_=new_hidden[(h_tile, b)][:])
+
+        def store_hidden_transposed(h_tile):
+            h_columns = slice(h_tile * P, (h_tile + 1) * P)
+            for b in range(BATCH):
+                bank = bank_pool.tile([P, BANK_WORDS], F32, name="bank")
+                for t in range(FRAMES // P):
+                    frames = slice(t * P, (t + 1) * P)
+                    nc.tensor.transpose(bank[:, frames], new_hidden[(h_tile, b)][:, frames], identity[:])
+                flipped = cell_tile("flipped")
+                copy_out = nc.scalar.copy if b == 0 else nc.vector.tensor_copy
+                copy_out(out=flipped[:], in_=bank[:, :FRAMES])
+                nc.sync.dma_start(
+                    out=out_0[b].rearrange("(t p) h -> p t h", p=P)[:, :, h_columns],
+                    in_=flipped[:].rearrange("p (t h) -> p t h", h=P),
+                )
+
+        def h_tile_closed_by(index):
+            if 0 <= index < len(rounds) and rounds[index][1][-1] == PASSES - 1:
+                return rounds[index][0]
+            return None
+
+        for step in range(LOAD_AHEAD):
+            load_chunk(step)
+        for index in range(len(rounds) + FLIP_LAG + 1):
+            if h_tile_closed_by(index - FLIP_LAG) is not None:
+                store_hidden_transposed(h_tile_closed_by(index - FLIP_LAG))
+            if index < len(rounds):
+                stage(index)
+            if 0 <= index - 1 < len(rounds):
+                multiply(index - 1)
+            if h_tile_closed_by(index - 2) is not None:
+                update_cell(h_tile_closed_by(index - 2))
+            if index < len(rounds):
+                quantise(index)
+            if index == 0:
+                prepare_small_inputs()
+            if h_tile_closed_by(index - 1) is not None:
+                activate_gates(h_tile_closed_by(index - 1))
+            if h_tile_closed_by(index - 2) is not None:
+                update_hidden(h_tile_closed_by(index - 2))

@@ -15,7 +15,6 @@ P = 128
 HALF = P // 2
 PACK = 4
 K_PASS = P * PACK
-PASS_WORDS = K_PASS // 2
 BANK_WORDS = 512
 
 BATCH, FRAMES, CHANNELS, HIDDEN = 2, 256, 7936, 256
@@ -28,8 +27,11 @@ H_TILES = HIDDEN // P
 
 CHUNK_PASSES = 2
 CHUNK_K = CHUNK_PASSES * K_PASS
+PLANE_WORDS = CHUNK_K // PACK
 CHUNKS = K // CHUNK_K
 LOAD_AHEAD = 3
+SORT_A_STEP = 4
+SORT_AHEAD = 2
 
 FREE_BANKS = 4
 OPERAND_BANKS = 2
@@ -37,6 +39,7 @@ BANK_TILES = 2
 BANK_COLUMNS = BANK_TILES * P
 
 IDLE_MATMULS = 3
+SMALL_INPUTS_ROUND = 8
 FLIP_LAG = 5
 
 FLOPS = 2 * GATES * HIDDEN * K * N
@@ -59,8 +62,10 @@ def tile_batchedlstm_k_kernel(
     with ExitStack() as ctx:
         ctx.enter_context(tc.manual_schedule())
         keep = ctx.enter_context(tc.tile_pool(name="keep", bufs=1))
-        x_raw_pool = ctx.enter_context(tc.tile_pool(name="x_raw", bufs=ROW_TILES * (LOAD_AHEAD + 1)))
-        w_raw_pool = ctx.enter_context(tc.tile_pool(name="w_raw", bufs=GATES * (LOAD_AHEAD + 1)))
+        x_raw_pool = ctx.enter_context(tc.tile_pool(name="x_raw", bufs=ROW_TILES * LOAD_AHEAD))
+        w_raw_pool = ctx.enter_context(tc.tile_pool(name="w_raw", bufs=GATES * LOAD_AHEAD))
+        x_sorted_pool = ctx.enter_context(tc.tile_pool(name="x_sorted", bufs=3 * ROW_TILES))
+        w_sorted_pool = ctx.enter_context(tc.tile_pool(name="w_sorted", bufs=3 * GATES))
         grouped_pool = ctx.enter_context(tc.tile_pool(name="grouped", bufs=2 * FREE_BANKS))
         w_mx_pool = ctx.enter_context(tc.tile_pool(name="w_mx", bufs=4))
         cell_pool = ctx.enter_context(tc.tile_pool(name="cell", bufs=H_TILES * BATCH))
@@ -121,8 +126,6 @@ def tile_batchedlstm_k_kernel(
                 width = min(CHUNK_K, CHANNELS - k0)
                 for r in range(ROW_TILES):
                     raw = x_raw_pool.tile([P, CHUNK_K], BF16, name="x_raw")
-                    if width < CHUNK_K:
-                        nc.gpsimd.memset(raw[:, width:], 0.0)
                     nc.sync.dma_start(
                         out=raw[:, :width], in_=x_rows[r * P : (r + 1) * P, k0 : k0 + width]
                     )
@@ -136,24 +139,64 @@ def tile_batchedlstm_k_kernel(
                 nc.sync.dma_start(out=raw[:], in_=cell_state.rearrange("b h f -> h b f")[h_rows])
                 cell_raw[h_tile] = raw
 
+        x_sorted = {}
+        w_sorted = {}
+        to_sort = []
+        for step in range(H_TILES * CHUNKS):
+            if step < CHUNKS:
+                to_sort += [(step, "x", r) for r in range(ROW_TILES)]
+            to_sort += [(step, "w", gate) for gate in range(GATES)]
+        sorted_count = [0]
+
+        def sort_tile():
+            step, operand, tile = to_sort[sorted_count[0]]
+            sorted_count[0] += 1
+            h_tile, chunk = divmod(step, CHUNKS)
+            words = PLANE_WORDS
+            if operand == "x":
+                raw = x_raw[(chunk, tile)]
+                planes = x_sorted_pool.tile([P, CHUNK_K], BF16, name="x_sorted")
+                x_sorted[(chunk, tile)] = planes
+                words = min(CHUNK_K, CHANNELS - chunk * CHUNK_K) // PACK
+            else:
+                raw = w_raw[(h_tile, chunk, tile)]
+                planes = w_sorted_pool.tile([P, CHUNK_K], BF16, name="w_sorted")
+                w_sorted[(h_tile, chunk, tile)] = planes
+            by_plane = planes[:].bitcast(F32).rearrange("p (u w) -> p u w", u=2)
+            if words < PLANE_WORDS:
+                nc.gpsimd.memset(by_plane[:, :, words:], 0.0)
+            nc.vector.tensor_copy(
+                out=by_plane[:, :, :words],
+                in_=raw[:, : words * PACK].bitcast(F32).rearrange("p (w u) -> p u w", u=2),
+            )
+            if sorted_count[0] == len(to_sort) or to_sort[sorted_count[0]][0] != step:
+                if step + LOAD_AHEAD < H_TILES * CHUNKS:
+                    load_chunk(step + LOAD_AHEAD)
+
+        def sort_until(count):
+            while sorted_count[0] < min(count, len(to_sort)):
+                sort_tile()
+
+        def sorted_by(round_index):
+            if round_index < PASSES:
+                return (ROW_TILES + GATES) * (round_index // CHUNK_PASSES + 1)
+            return (ROW_TILES + GATES) * CHUNKS + GATES * (round_index - PASSES + 1)
+
         staged = {}
 
-        def transpose_operand(index, sources, first_word, codes, scales, vector_helps):
+        def transpose_operand(index, sources, first_word, codes, scales):
             for half in range(OPERAND_BANKS):
                 bank = bank_pool.tile([P, BANK_WORDS], F32, name="bank")
                 planes = bank[:].rearrange("p (s u n) -> p s u n", s=BANK_TILES, u=2)
                 for s in range(BANK_TILES):
                     words = sources[BANK_TILES * half + s][:].bitcast(F32)
                     for u in range(2):
-                        w0 = first_word + u
-                        nc.tensor.transpose(
-                            planes[:, s, u, :], words[:, w0 : first_word + PASS_WORDS : 2], identity[:]
-                        )
+                        w0 = u * PLANE_WORDS + first_word
+                        nc.tensor.transpose(planes[:, s, u, :], words[:, w0 : w0 + P], identity[:])
                 grouped = grouped_pool.tile(
                     [P, BANK_COLUMNS * PACK], BF16, align_bytes=64, name="grouped"
                 )
-                copy_out = nc.vector.tensor_copy if vector_helps and half == 1 else nc.scalar.copy
-                copy_out(
+                nc.scalar.copy(
                     out=grouped[:].bitcast(F32).rearrange("p (s n u) -> p s n u", s=BANK_TILES, u=2),
                     in_=planes.rearrange("p s u n -> p s n u"),
                 )
@@ -167,13 +210,10 @@ def tile_batchedlstm_k_kernel(
                 for s in range(BANK_TILES):
                     words = sources[BANK_TILES * half + s][:].bitcast(F32)
                     for u in range(2):
-                        w0 = first_word + u
-                        nc.tensor.transpose(
-                            planes[:, s, u, :], words[:, w0 : first_word + PASS_WORDS : 2], identity[:]
-                        )
+                        w0 = u * PLANE_WORDS + first_word
+                        nc.tensor.transpose(planes[:, s, u, :], words[:, w0 : w0 + P], identity[:])
                 columns = slice(half * BANK_COLUMNS * PACK, (half + 1) * BANK_COLUMNS * PACK)
-                copy_out = nc.vector.tensor_copy if half == 1 else nc.scalar.copy
-                copy_out(
+                nc.scalar.copy(
                     out=last_xh[:HALF, columns]
                     .bitcast(F32)
                     .rearrange("p (s n u) -> p s n u", s=BANK_TILES, u=2),
@@ -191,33 +231,34 @@ def tile_batchedlstm_k_kernel(
             staged[index] = []
             for g in passes:
                 chunk, pass_in_chunk = divmod(g, CHUNK_PASSES)
-                first_word = pass_in_chunk * PASS_WORDS
+                first_word = pass_in_chunk * P
                 if h_tile == 0:
-                    sources = [x_raw[(chunk, r)] for r in range(ROW_TILES)]
+                    sources = [x_sorted[(chunk, r)] for r in range(ROW_TILES)]
                     x_codes[g] = keep.tile([P, N], U32, align_bytes=64, name="x_codes%d" % g)
                     x_scales[g] = keep.tile([P, N], U8, align_bytes=64, name="x_scales%d" % g)
                     if g < PASSES - 1:
-                        transpose_operand(index, sources, first_word, x_codes[g], x_scales[g], True)
+                        transpose_operand(index, sources, first_word, x_codes[g], x_scales[g])
                     else:
                         transpose_last_xh(index, sources, first_word, x_codes[g], x_scales[g])
                     if index == 0:
                         hold_clock()
-                step = h_tile * CHUNKS + chunk
-                if pass_in_chunk == 0 and step + LOAD_AHEAD < H_TILES * CHUNKS:
-                    load_chunk(step + LOAD_AHEAD)
-                sources = [w_raw[(h_tile, chunk, gate)] for gate in range(GATES)]
+                sources = [w_sorted[(h_tile, chunk, gate)] for gate in range(GATES)]
                 codes = w_mx_pool.tile([P, GATES * P], U32, align_bytes=64, name="w_codes")
                 scales = w_mx_pool.tile([P, GATES * P], U8, align_bytes=64, name="w_scales")
                 w_codes[(h_tile, g)] = codes
                 w_scales[(h_tile, g)] = scales
-                first_operand = len(staged[index]) == 0
-                transpose_operand(index, sources, first_word, codes, scales, first_operand)
+                transpose_operand(index, sources, first_word, codes, scales)
                 if index == 0:
                     hold_clock()
 
         def quantise(index):
-            for grouped, codes, scales in staged[index]:
+            target = sorted_by(index + SORT_AHEAD)
+            if index + SORT_AHEAD + 1 < PASSES:
+                target = max(target, sorted_by(index + SORT_AHEAD + 1) - SORT_A_STEP)
+            missing = max(0, min(target, len(to_sort)) - sorted_count[0])
+            for position, (grouped, codes, scales) in enumerate(staged[index]):
                 nc.vector.quantize_mx(out=codes.bitcast(FP8X4), scales=scales, in_=grouped)
+                sort_until(target - missing + missing * (position + 1) // len(staged[index]))
 
         acc = {}
 
@@ -321,6 +362,7 @@ def tile_batchedlstm_k_kernel(
 
         for step in range(LOAD_AHEAD):
             load_chunk(step)
+        sort_until(sorted_by(0))
         for index in range(len(rounds) + FLIP_LAG + 1):
             if h_tile_closed_by(index - FLIP_LAG) is not None:
                 store_hidden_transposed(h_tile_closed_by(index - FLIP_LAG))
@@ -332,7 +374,7 @@ def tile_batchedlstm_k_kernel(
                 update_cell(h_tile_closed_by(index - 2))
             if index < len(rounds):
                 quantise(index)
-            if index == 0:
+            if index == SMALL_INPUTS_ROUND:
                 prepare_small_inputs()
             if h_tile_closed_by(index - 1) is not None:
                 activate_gates(h_tile_closed_by(index - 1))

@@ -30,8 +30,10 @@ CHUNK_K = CHUNK_PASSES * K_PASS
 PLANE_WORDS = CHUNK_K // PACK
 CHUNKS = K // CHUNK_K
 LOAD_AHEAD = 3
-SORT_A_STEP = 4
-SORT_AHEAD = 2
+HEAD_CHUNKS = 2
+SORT_A_STEP = 4 * CHUNK_PASSES
+HEAD_STEPS = 2
+SORT_LEAD = 14 * CHUNK_PASSES
 
 FREE_BANKS = 4
 OPERAND_BANKS = 2
@@ -68,6 +70,7 @@ def tile_batchedlstm_k_kernel(
         w_sorted_pool = ctx.enter_context(tc.tile_pool(name="w_sorted", bufs=3 * GATES))
         grouped_pool = ctx.enter_context(tc.tile_pool(name="grouped", bufs=2 * FREE_BANKS))
         w_mx_pool = ctx.enter_context(tc.tile_pool(name="w_mx", bufs=4))
+        w_late_pool = ctx.enter_context(tc.tile_pool(name="w_late", bufs=PASSES))
         cell_pool = ctx.enter_context(tc.tile_pool(name="cell", bufs=H_TILES * BATCH))
         acc_pool = ctx.enter_context(tc.psum_pool(name="acc", bufs=1))
         bank_pool = ctx.enter_context(tc.psum_pool(name="bank", bufs=FREE_BANKS))
@@ -79,30 +82,38 @@ def tile_batchedlstm_k_kernel(
 
         bias_rows = keep.tile([P, P], BF16, name="bias_rows")
         nc.vector.memset(bias_rows[:], 0.0)
-        for gate in range(GATES):
-            nc.scalar.dma_start(
-                out=bias_rows[gate * H_TILES : (gate + 1) * H_TILES, :],
-                in_=biases[gate].rearrange("(t p) -> t p", p=P),
-            )
         bias_columns = keep.tile([P, GATES * H_TILES], F32, name="bias_columns")
 
         hidden_raw = keep.tile([P, BATCH, PACK * FRAMES], BF16, name="hidden_raw")
-        nc.scalar.dma_start(
-            out=hidden_raw[HALF:, :, :],
-            in_=hidden_state.rearrange("b (p t) f -> p b (t f)", t=PACK),
-        )
+
+        def load_small_inputs():
+            for gate in range(GATES):
+                nc.sync.dma_start(
+                    out=bias_rows[gate * H_TILES : (gate + 1) * H_TILES, :],
+                    in_=biases[gate].rearrange("(t p) -> t p", p=P),
+                )
+            nc.sync.dma_start(
+                out=hidden_raw[HALF:, :, :],
+                in_=hidden_state.rearrange("b (p t) f -> p b (t f)", t=PACK),
+            )
+
         last_xh = keep.tile([P, N * PACK], BF16, align_bytes=64, name="last_xh")
 
         warm = keep.tile([P, 1], F32, name="warm")
         nc.vector.memset(warm[:], 0.0)
         nc.scalar.activation(out=warm[:], in_=warm[:], func=ACT.Sigmoid)
 
-        def prepare_small_inputs():
-            bias_rows_f32 = keep.tile([P, P], F32, name="bias_rows_f32")
+        bias_rows_f32 = keep.tile([P, P], F32, name="bias_rows_f32")
+
+        def widen_biases():
             nc.vector.tensor_copy(out=bias_rows_f32[:], in_=bias_rows[:])
+
+        def turn_biases():
             bank = bank_pool.tile([P, BANK_WORDS], F32, name="bank")
             nc.tensor.transpose(bank[:, :P], bias_rows_f32[:], identity[:])
-            nc.vector.tensor_copy(out=bias_columns[:], in_=bank[:, : GATES * H_TILES])
+            nc.scalar.copy(out=bias_columns[:], in_=bank[:, : GATES * H_TILES])
+
+        def prepare_hidden_state():
             nc.vector.tensor_copy(
                 out=last_xh[HALF:, :].rearrange("p (b f t) -> p b f t", b=BATCH, t=PACK),
                 in_=hidden_raw[HALF:, :, :].rearrange("p b (t f) -> p b f t", t=PACK),
@@ -118,22 +129,37 @@ def tile_batchedlstm_k_kernel(
         w_raw = {}
         cell_raw = {}
 
+        def pieces(step):
+            if step < HEAD_CHUNKS:
+                return [(g, g + 1) for g in range(CHUNK_PASSES)]
+            return [(0, CHUNK_PASSES)]
+
         def load_chunk(step):
             h_tile, chunk = divmod(step, CHUNKS)
             h_rows = slice(h_tile * P, (h_tile + 1) * P)
             k0 = chunk * CHUNK_K
+            width = min(CHUNK_K, CHANNELS - k0)
             if h_tile == 0:
-                width = min(CHUNK_K, CHANNELS - k0)
                 for r in range(ROW_TILES):
-                    raw = x_raw_pool.tile([P, CHUNK_K], BF16, name="x_raw")
-                    nc.sync.dma_start(
-                        out=raw[:, :width], in_=x_rows[r * P : (r + 1) * P, k0 : k0 + width]
-                    )
-                    x_raw[(chunk, r)] = raw
+                    x_raw[(chunk, r)] = x_raw_pool.tile([P, CHUNK_K], BF16, name="x_raw")
             for gate in range(GATES):
-                raw = w_raw_pool.tile([P, CHUNK_K], BF16, name="w_raw")
-                nc.sync.dma_start(out=raw[:], in_=weights[gate][h_rows, k0 : k0 + CHUNK_K])
-                w_raw[(h_tile, chunk, gate)] = raw
+                w_raw[(h_tile, chunk, gate)] = w_raw_pool.tile([P, CHUNK_K], BF16, name="w_raw")
+            for first, last in pieces(step):
+                if h_tile == 0:
+                    piece = slice(first * K_PASS, min(last * K_PASS, width))
+                    for r in range(ROW_TILES):
+                        nc.sync.dma_start(
+                            out=x_raw[(chunk, r)][:, piece],
+                            in_=x_rows[r * P : (r + 1) * P, k0 + piece.start : k0 + piece.stop],
+                        )
+                piece = slice(first * K_PASS, last * K_PASS)
+                for gate in range(GATES):
+                    nc.sync.dma_start(
+                        out=w_raw[(h_tile, chunk, gate)][:, piece],
+                        in_=weights[gate][h_rows, k0 + piece.start : k0 + piece.stop],
+                    )
+            if step == LOAD_AHEAD:
+                load_small_inputs()
             if chunk == CHUNKS - 1:
                 raw = cell_pool.tile([P, BATCH, FRAMES], BF16, name="cell_raw")
                 nc.sync.dma_start(out=raw[:], in_=cell_state.rearrange("b h f -> h b f")[h_rows])
@@ -143,44 +169,56 @@ def tile_batchedlstm_k_kernel(
         w_sorted = {}
         to_sort = []
         for step in range(H_TILES * CHUNKS):
-            if step < CHUNKS:
-                to_sort += [(step, "x", r) for r in range(ROW_TILES)]
-            to_sort += [(step, "w", gate) for gate in range(GATES)]
-        sorted_count = [0]
+            for first, last in pieces(step):
+                if step < CHUNKS:
+                    to_sort += [(step, "x", r, first, last) for r in range(ROW_TILES)]
+                to_sort += [(step, "w", gate, first, last) for gate in range(GATES)]
+        sorted_passes = [0]
 
         def sort_tile():
-            step, operand, tile = to_sort[sorted_count[0]]
-            sorted_count[0] += 1
+            step, operand, tile, first, last = to_sort.pop(0)
+            sorted_passes[0] += last - first
             h_tile, chunk = divmod(step, CHUNKS)
-            words = PLANE_WORDS
+            words = slice(first * P, last * P)
             if operand == "x":
                 raw = x_raw[(chunk, tile)]
-                planes = x_sorted_pool.tile([P, CHUNK_K], BF16, name="x_sorted")
-                x_sorted[(chunk, tile)] = planes
-                words = min(CHUNK_K, CHANNELS - chunk * CHUNK_K) // PACK
+                if first == 0:
+                    x_sorted[(chunk, tile)] = x_sorted_pool.tile([P, CHUNK_K], BF16, name="x_sorted")
+                planes = x_sorted[(chunk, tile)]
+                words = slice(words.start, min(words.stop, (CHANNELS - chunk * CHUNK_K) // PACK))
             else:
                 raw = w_raw[(h_tile, chunk, tile)]
-                planes = w_sorted_pool.tile([P, CHUNK_K], BF16, name="w_sorted")
-                w_sorted[(h_tile, chunk, tile)] = planes
+                if first == 0:
+                    w_sorted[(h_tile, chunk, tile)] = w_sorted_pool.tile(
+                        [P, CHUNK_K], BF16, name="w_sorted"
+                    )
+                planes = w_sorted[(h_tile, chunk, tile)]
             by_plane = planes[:].bitcast(F32).rearrange("p (u w) -> p u w", u=2)
-            if words < PLANE_WORDS:
-                nc.gpsimd.memset(by_plane[:, :, words:], 0.0)
+            if words.stop < last * P:
+                nc.gpsimd.memset(by_plane[:, :, words.stop :], 0.0)
             nc.vector.tensor_copy(
-                out=by_plane[:, :, :words],
-                in_=raw[:, : words * PACK].bitcast(F32).rearrange("p (w u) -> p u w", u=2),
+                out=by_plane[:, :, words],
+                in_=raw[:].bitcast(F32).rearrange("p (w u) -> p u w", u=2)[:, :, words],
             )
-            if sorted_count[0] == len(to_sort) or to_sort[sorted_count[0]][0] != step:
+            if len(to_sort) == 0 or to_sort[0][0] != step:
                 if step + LOAD_AHEAD < H_TILES * CHUNKS:
                     load_chunk(step + LOAD_AHEAD)
 
         def sort_until(count):
-            while sorted_count[0] < min(count, len(to_sort)):
+            while sorted_passes[0] < count and len(to_sort) > 0:
                 sort_tile()
 
         def sorted_by(round_index):
             if round_index < PASSES:
-                return (ROW_TILES + GATES) * (round_index // CHUNK_PASSES + 1)
-            return (ROW_TILES + GATES) * CHUNKS + GATES * (round_index - PASSES + 1)
+                return (ROW_TILES + GATES) * (round_index + 1)
+            h_passes = CHUNK_PASSES * (round_index - PASSES + 1)
+            return (ROW_TILES + GATES) * PASSES + GATES * h_passes
+
+        def sort_target(index):
+            if index < HEAD_STEPS:
+                return sorted_by(index + 1)
+            target = SORT_LEAD + SORT_A_STEP * index
+            return target if index + 2 < PASSES else min(target, sorted_by(index + 2))
 
         staged = {}
 
@@ -200,8 +238,7 @@ def tile_batchedlstm_k_kernel(
                     out=grouped[:].bitcast(F32).rearrange("p (s n u) -> p s n u", s=BANK_TILES, u=2),
                     in_=planes.rearrange("p s u n -> p s n u"),
                 )
-                columns = slice(half * BANK_COLUMNS, (half + 1) * BANK_COLUMNS)
-                staged[index].append((grouped[:], codes[:, columns], scales[:, columns]))
+                staged[index].append((grouped[:], codes[half], scales[half]))
 
         def transpose_last_xh(index, sources, first_word, codes, scales):
             for half in range(OPERAND_BANKS):
@@ -237,67 +274,96 @@ def tile_batchedlstm_k_kernel(
                     x_codes[g] = keep.tile([P, N], U32, align_bytes=64, name="x_codes%d" % g)
                     x_scales[g] = keep.tile([P, N], U8, align_bytes=64, name="x_scales%d" % g)
                     if g < PASSES - 1:
-                        transpose_operand(index, sources, first_word, x_codes[g], x_scales[g])
+                        columns = [
+                            slice(half * BANK_COLUMNS, (half + 1) * BANK_COLUMNS)
+                            for half in range(OPERAND_BANKS)
+                        ]
+                        transpose_operand(
+                            index,
+                            sources,
+                            first_word,
+                            [x_codes[g][:, c] for c in columns],
+                            [x_scales[g][:, c] for c in columns],
+                        )
                     else:
                         transpose_last_xh(index, sources, first_word, x_codes[g], x_scales[g])
                     if index == 0:
                         hold_clock()
                 sources = [w_sorted[(h_tile, chunk, gate)] for gate in range(GATES)]
-                codes = w_mx_pool.tile([P, GATES * P], U32, align_bytes=64, name="w_codes")
-                scales = w_mx_pool.tile([P, GATES * P], U8, align_bytes=64, name="w_scales")
+                codes, scales = [], []
+                for pool in (w_mx_pool, w_late_pool):
+                    codes.append(pool.tile([P, BANK_COLUMNS], U32, align_bytes=64, name="w_codes"))
+                    scales.append(pool.tile([P, BANK_COLUMNS], U8, align_bytes=64, name="w_scales"))
                 w_codes[(h_tile, g)] = codes
                 w_scales[(h_tile, g)] = scales
-                transpose_operand(index, sources, first_word, codes, scales)
+                transpose_operand(
+                    index, sources, first_word, [c[:] for c in codes], [c[:] for c in scales]
+                )
                 if index == 0:
                     hold_clock()
 
         def quantise(index):
-            target = sorted_by(index + SORT_AHEAD)
-            if index + SORT_AHEAD + 1 < PASSES:
-                target = max(target, sorted_by(index + SORT_AHEAD + 1) - SORT_A_STEP)
-            missing = max(0, min(target, len(to_sort)) - sorted_count[0])
+            done = sorted_passes[0]
+            missing = max(0, sort_target(index) - done)
             for position, (grouped, codes, scales) in enumerate(staged[index]):
                 nc.vector.quantize_mx(out=codes.bitcast(FP8X4), scales=scales, in_=grouped)
-                sort_until(target - missing + missing * (position + 1) // len(staged[index]))
+                sort_until(done + missing * (position + 1) // len(staged[index]))
 
         acc = {}
 
+        def gate_pass(out, h_tile, gate, g, columns):
+            half, gate_in_half = divmod(gate, BANK_TILES)
+            rows = slice(gate_in_half * P, (gate_in_half + 1) * P)
+            nc.tensor.matmul_mx(
+                out=out,
+                lhsT=w_codes[(h_tile, g)][half][:, rows].bitcast(FP8X4),
+                lhsT_scale=w_scales[(h_tile, g)][half][:, rows],
+                rhs=x_codes[g][:, columns].bitcast(FP8X4),
+                rhs_scale=x_scales[g][:, columns],
+                start=(g == 0),
+                stop=(g == PASSES - 1),
+            )
+
+        banks = {}
+
         def multiply(index):
             h_tile, passes = rounds[index]
-            for gate in range(GATES):
+            for gate in range(GATES if h_tile < H_TILES - 1 else GATES - 1):
                 if passes[0] == 0:
-                    acc[(h_tile, gate)] = acc_pool.tile([P, N], F32, name="acc%d" % gate)
-                gate_columns = slice(gate * P, (gate + 1) * P)
+                    banks[gate] = acc_pool.tile([P, N], F32, name="acc%d" % gate)
+                    for b in range(BATCH):
+                        acc[(h_tile, gate, b)] = banks[gate][:, b * FRAMES : (b + 1) * FRAMES]
                 for g in passes:
-                    nc.tensor.matmul_mx(
-                        out=acc[(h_tile, gate)][:],
-                        lhsT=w_codes[(h_tile, g)][:, gate_columns].bitcast(FP8X4),
-                        lhsT_scale=w_scales[(h_tile, g)][:, gate_columns],
-                        rhs=x_codes[g][:].bitcast(FP8X4),
-                        rhs_scale=x_scales[g][:],
-                        start=(g == 0),
-                        stop=(g == PASSES - 1),
-                    )
+                    gate_pass(banks[gate][:], h_tile, gate, g, slice(0, N))
+
+        def multiply_late():
+            h_tile, gate = H_TILES - 1, GATES - 1
+            for b in range(BATCH):
+                bank = bank_pool.tile([P, BANK_WORDS], F32, name="bank")
+                acc[(h_tile, gate, b)] = bank[:, :FRAMES]
+                for g in range(PASSES):
+                    gate_pass(bank[:, :FRAMES], h_tile, gate, g, slice(b * FRAMES, (b + 1) * FRAMES))
 
         activated = {}
         new_cell = {}
+        squashed = {}
         new_hidden = {}
+        flipped = {}
 
         def cell_tile(name):
             return cell_pool.tile([P, FRAMES], F32, name=name)
 
-        def activate_gates(h_tile):
-            for gate in range(GATES):
-                bias_column = gate * H_TILES + h_tile
-                for b in range(BATCH):
-                    activated[(h_tile, gate, b)] = cell_tile("gate%d" % gate)
-                    nc.scalar.activation(
-                        out=activated[(h_tile, gate, b)][:],
-                        in_=acc[(h_tile, gate)][:, b * FRAMES : (b + 1) * FRAMES],
-                        func=gate_functions[gate],
-                        bias=bias_columns[:, bias_column : bias_column + 1],
-                        scale=1.0,
-                    )
+        def activate_gate(h_tile, gate, b, columns=slice(0, FRAMES)):
+            if columns.start == 0:
+                activated[(h_tile, gate, b)] = cell_tile("gate%d" % gate)
+            bias_column = gate * H_TILES + h_tile
+            nc.scalar.activation(
+                out=activated[(h_tile, gate, b)][:, columns],
+                in_=acc[(h_tile, gate, b)][:, columns],
+                func=gate_functions[gate],
+                bias=bias_columns[:, bias_column : bias_column + 1],
+                scale=1.0,
+            )
 
         def update_cell(h_tile):
             h_rows = slice(h_tile * P, (h_tile + 1) * P)
@@ -324,59 +390,93 @@ def tile_batchedlstm_k_kernel(
                 )
                 nc.sync.dma_start(out=out_2[b, h_rows, :], in_=new_cell[(h_tile, b)][:])
 
-        def update_hidden(h_tile):
-            h_rows = slice(h_tile * P, (h_tile + 1) * P)
-            squashed = {}
+        def squash_cell(h_tile):
             for b in range(BATCH):
-                squashed[b] = cell_tile("squashed")
-                nc.scalar.activation(out=squashed[b][:], in_=new_cell[(h_tile, b)][:], func=ACT.Tanh)
-            for b in range(BATCH):
+                squashed[(h_tile, b)] = cell_tile("squashed")
+                nc.scalar.activation(
+                    out=squashed[(h_tile, b)][:], in_=new_cell[(h_tile, b)][:], func=ACT.Tanh
+                )
+
+        def update_hidden(h_tile, b, columns=slice(0, FRAMES)):
+            if columns.start == 0:
                 new_hidden[(h_tile, b)] = cell_tile("new_hidden")
-                nc.vector.tensor_tensor(
-                    out=new_hidden[(h_tile, b)][:],
-                    in0=squashed[b][:],
-                    in1=activated[(h_tile, 3, b)][:],
-                    op=ALU.mult,
-                )
-                nc.sync.dma_start(out=out_1[b, h_rows, :], in_=new_hidden[(h_tile, b)][:])
+            nc.vector.tensor_tensor(
+                out=new_hidden[(h_tile, b)][:, columns],
+                in0=squashed[(h_tile, b)][:, columns],
+                in1=activated[(h_tile, GATES - 1, b)][:, columns],
+                op=ALU.mult,
+            )
 
-        def store_hidden_transposed(h_tile):
+        def store_hidden(h_tile, b):
+            h_rows = slice(h_tile * P, (h_tile + 1) * P)
+            nc.sync.dma_start(out=out_1[b, h_rows, :], in_=new_hidden[(h_tile, b)][:])
+
+        def flip_hidden(h_tile, b):
+            bank = bank_pool.tile([P, BANK_WORDS], F32, name="bank")
+            for columns in f_tiles:
+                nc.tensor.transpose(bank[:, columns], new_hidden[(h_tile, b)][:, columns], identity[:])
+            flipped[(h_tile, b)] = cell_tile("flipped")
+            return bank
+
+        def store_flipped(h_tile, b, tiles):
             h_columns = slice(h_tile * P, (h_tile + 1) * P)
-            for b in range(BATCH):
-                bank = bank_pool.tile([P, BANK_WORDS], F32, name="bank")
-                for t in range(FRAMES // P):
-                    frames = slice(t * P, (t + 1) * P)
-                    nc.tensor.transpose(bank[:, frames], new_hidden[(h_tile, b)][:, frames], identity[:])
-                flipped = cell_tile("flipped")
-                copy_out = nc.scalar.copy if b == 0 else nc.vector.tensor_copy
-                copy_out(out=flipped[:], in_=bank[:, :FRAMES])
-                nc.sync.dma_start(
-                    out=out_0[b].rearrange("(t p) h -> p t h", p=P)[:, :, h_columns],
-                    in_=flipped[:].rearrange("p (t h) -> p t h", h=P),
-                )
+            nc.sync.dma_start(
+                out=out_0[b].rearrange("(t p) h -> p t h", p=P)[:, tiles, h_columns],
+                in_=flipped[(h_tile, b)][:].rearrange("p (t h) -> p t h", h=P)[:, tiles, :],
+            )
 
-        def h_tile_closed_by(index):
-            if 0 <= index < len(rounds) and rounds[index][1][-1] == PASSES - 1:
-                return rounds[index][0]
-            return None
+        f_tiles = [slice(t * P, (t + 1) * P) for t in range(FRAMES // P)]
+
+        def finish_last_tile():
+            h_tile = H_TILES - 1
+            for gate in range(GATES - 1):
+                for b in range(BATCH):
+                    activate_gate(h_tile, gate, b)
+            update_cell(h_tile)
+            squash_cell(h_tile)
+            for b in range(BATCH):
+                for columns in f_tiles:
+                    activate_gate(h_tile, GATES - 1, b, columns)
+                    update_hidden(h_tile, b, columns)
+                store_hidden(h_tile, b)
+            turned = [flip_hidden(h_tile, b) for b in range(BATCH)]
+            nc.scalar.copy(out=flipped[(h_tile, 0)][:], in_=turned[0][:, :FRAMES])
+            store_flipped(h_tile, 0, slice(0, 2))
+            for t, columns in enumerate(f_tiles):
+                nc.vector.tensor_copy(out=flipped[(h_tile, 1)][:, columns], in_=turned[1][:, columns])
+                store_flipped(h_tile, 1, slice(t, t + 1))
 
         for step in range(LOAD_AHEAD):
             load_chunk(step)
         sort_until(sorted_by(0))
-        for index in range(len(rounds) + FLIP_LAG + 1):
-            if h_tile_closed_by(index - FLIP_LAG) is not None:
-                store_hidden_transposed(h_tile_closed_by(index - FLIP_LAG))
+        for index in range(len(rounds) + 1):
+            if index == PASSES - 1 + FLIP_LAG:
+                for b in range(BATCH):
+                    bank = flip_hidden(0, b)
+                    nc.scalar.copy(out=flipped[(0, b)][:], in_=bank[:, :FRAMES])
+                    store_flipped(0, b, slice(0, 2))
+            if index == SMALL_INPUTS_ROUND + 2:
+                turn_biases()
             if index < len(rounds):
                 stage(index)
-            if 0 <= index - 1 < len(rounds):
+            if index > 0:
                 multiply(index - 1)
-            if h_tile_closed_by(index - 2) is not None:
-                update_cell(h_tile_closed_by(index - 2))
+            if index == PASSES + 1:
+                update_cell(0)
             if index < len(rounds):
                 quantise(index)
             if index == SMALL_INPUTS_ROUND:
-                prepare_small_inputs()
-            if h_tile_closed_by(index - 1) is not None:
-                activate_gates(h_tile_closed_by(index - 1))
-            if h_tile_closed_by(index - 2) is not None:
-                update_hidden(h_tile_closed_by(index - 2))
+                widen_biases()
+            if index == PASSES - 2:
+                prepare_hidden_state()
+            if index == PASSES:
+                for gate in range(GATES):
+                    for b in range(BATCH):
+                        activate_gate(0, gate, b)
+            if index == PASSES + 1:
+                squash_cell(0)
+                for b in range(BATCH):
+                    update_hidden(0, b)
+                    store_hidden(0, b)
+        multiply_late()
+        finish_last_tile()

@@ -27,7 +27,7 @@ H_TILES = HIDDEN // P
 
 CHUNK_PASSES = 2
 CHUNK_K = CHUNK_PASSES * K_PASS
-PLANE_WORDS = CHUNK_K // PACK
+RUN = 8
 CHUNKS = K // CHUNK_K
 LOAD_AHEAD = 3
 HEAD_CHUNKS = 2
@@ -130,7 +130,7 @@ def tile_batchedlstm_k_kernel(
         cell_raw = {}
 
         def pieces(step):
-            if step < HEAD_CHUNKS:
+            if step < HEAD_CHUNKS or step % CHUNKS == CHUNKS - 1:
                 return [(g, g + 1) for g in range(CHUNK_PASSES)]
             return [(0, CHUNK_PASSES)]
 
@@ -179,13 +179,11 @@ def tile_batchedlstm_k_kernel(
             step, operand, tile, first, last = to_sort.pop(0)
             sorted_passes[0] += last - first
             h_tile, chunk = divmod(step, CHUNKS)
-            words = slice(first * P, last * P)
             if operand == "x":
                 raw = x_raw[(chunk, tile)]
                 if first == 0:
                     x_sorted[(chunk, tile)] = x_sorted_pool.tile([P, CHUNK_K], BF16, name="x_sorted")
                 planes = x_sorted[(chunk, tile)]
-                words = slice(words.start, min(words.stop, (CHANNELS - chunk * CHUNK_K) // PACK))
             else:
                 raw = w_raw[(h_tile, chunk, tile)]
                 if first == 0:
@@ -193,13 +191,26 @@ def tile_batchedlstm_k_kernel(
                         [P, CHUNK_K], BF16, name="w_sorted"
                     )
                 planes = w_sorted[(h_tile, chunk, tile)]
-            by_plane = planes[:].bitcast(F32).rearrange("p (u w) -> p u w", u=2)
-            if words.stop < last * P:
-                nc.gpsimd.memset(by_plane[:, :, words.stop :], 0.0)
-            nc.vector.tensor_copy(
-                out=by_plane[:, :, words],
-                in_=raw[:].bitcast(F32).rearrange("p (w u) -> p u w", u=2)[:, :, words],
-            )
+            by_plane = planes[:].bitcast(F32).rearrange("p (m u w) -> p m u w", u=2, w=P)
+            k0 = chunk * CHUNK_K + first * K_PASS
+            width = (last - first) * K_PASS
+            if operand == "x":
+                width = min(width, CHANNELS - k0)
+            words = raw[:, first * K_PASS : first * K_PASS + width].bitcast(F32)
+            if last - first == CHUNK_PASSES:
+                nc.vector.tensor_copy(
+                    out=by_plane.rearrange("p m u (q i) -> p m u q i", i=RUN),
+                    in_=words.rearrange("p (m q u i) -> p m u q i", m=CHUNK_PASSES, u=2, i=RUN),
+                )
+            else:
+                run = RUN if k0 < K - K_PASS else 1
+                n = width // PACK
+                if n < P:
+                    nc.gpsimd.memset(by_plane[:, first, :, n:], 0.0)
+                nc.vector.tensor_copy(
+                    out=by_plane[:, first, :, :n].rearrange("p u (h q i) -> p h u q i", h=2, i=run),
+                    in_=words.rearrange("p (h q u i) -> p h u q i", h=2, u=2, i=run),
+                )
             if len(to_sort) == 0 or to_sort[0][0] != step:
                 if step + LOAD_AHEAD < H_TILES * CHUNKS:
                     load_chunk(step + LOAD_AHEAD)
@@ -229,7 +240,7 @@ def tile_batchedlstm_k_kernel(
                 for s in range(BANK_TILES):
                     words = sources[BANK_TILES * half + s][:].bitcast(F32)
                     for u in range(2):
-                        w0 = u * PLANE_WORDS + first_word
+                        w0 = first_word + u * P
                         nc.tensor.transpose(planes[:, s, u, :], words[:, w0 : w0 + P], identity[:])
                 grouped = grouped_pool.tile(
                     [P, BANK_COLUMNS * PACK], BF16, align_bytes=64, name="grouped"
@@ -247,7 +258,7 @@ def tile_batchedlstm_k_kernel(
                 for s in range(BANK_TILES):
                     words = sources[BANK_TILES * half + s][:].bitcast(F32)
                     for u in range(2):
-                        w0 = u * PLANE_WORDS + first_word
+                        w0 = first_word + u * P
                         nc.tensor.transpose(planes[:, s, u, :], words[:, w0 : w0 + P], identity[:])
                 columns = slice(half * BANK_COLUMNS * PACK, (half + 1) * BANK_COLUMNS * PACK)
                 nc.scalar.copy(
@@ -268,7 +279,7 @@ def tile_batchedlstm_k_kernel(
             staged[index] = []
             for g in passes:
                 chunk, pass_in_chunk = divmod(g, CHUNK_PASSES)
-                first_word = pass_in_chunk * P
+                first_word = pass_in_chunk * 2 * P
                 if h_tile == 0:
                     sources = [x_sorted[(chunk, r)] for r in range(ROW_TILES)]
                     x_codes[g] = keep.tile([P, N], U32, align_bytes=64, name="x_codes%d" % g)

@@ -27,6 +27,7 @@ H_TILES = HIDDEN // P
 
 CHUNK_PASSES = 2
 CHUNK_K = CHUNK_PASSES * K_PASS
+COLUMN_RUN = 4
 RUN = 8
 CHUNKS = K // CHUNK_K
 LOAD_AHEAD = 3
@@ -40,6 +41,7 @@ OPERAND_BANKS = 2
 BANK_TILES = 2
 BANK_COLUMNS = BANK_TILES * P
 
+FIRST_IDLE_MATMULS = 4
 IDLE_MATMULS = 3
 SMALL_INPUTS_ROUND = 8
 FLIP_LAG = 5
@@ -75,10 +77,10 @@ def tile_batchedlstm_k_kernel(
         acc_pool = ctx.enter_context(tc.psum_pool(name="acc", bufs=1))
         bank_pool = ctx.enter_context(tc.psum_pool(name="bank", bufs=FREE_BANKS))
 
-        identity = keep.tile([P, P], F32, name="identity")
-        make_identity(nc, identity[:])
         zeros = keep.tile([P, N], BF16, name="zeros")
         nc.vector.memset(zeros[:], 0.0)
+        identity = keep.tile([P, P], F32, name="identity")
+        make_identity(nc, identity[:])
 
         bias_rows = keep.tile([P, P], BF16, name="bias_rows")
         nc.vector.memset(bias_rows[:], 0.0)
@@ -121,8 +123,8 @@ def tile_batchedlstm_k_kernel(
 
         idle_bank = acc_pool.tile([P, N], F32, name="acc0")
 
-        def hold_clock():
-            for repeat in range(IDLE_MATMULS):
+        def hold_clock(repeats):
+            for repeat in range(repeats):
                 nc.tensor.matmul(idle_bank[:], lhsT=zeros[:, :P], rhs=zeros[:], start=True, stop=True)
 
         x_raw = {}
@@ -236,36 +238,36 @@ def tile_batchedlstm_k_kernel(
         def transpose_operand(index, sources, first_word, codes, scales):
             for half in range(OPERAND_BANKS):
                 bank = bank_pool.tile([P, BANK_WORDS], F32, name="bank")
-                planes = bank[:].rearrange("p (s u n) -> p s u n", s=BANK_TILES, u=2)
+                planes = bank[:].rearrange("p (u n) -> p u n", u=2)
                 for s in range(BANK_TILES):
                     words = sources[BANK_TILES * half + s][:].bitcast(F32)
                     for u in range(2):
                         w0 = first_word + u * P
-                        nc.tensor.transpose(planes[:, s, u, :], words[:, w0 : w0 + P], identity[:])
+                        nc.tensor.transpose(planes[:, u, s * P : (s + 1) * P], words[:, w0 : w0 + P], identity[:])
                 grouped = grouped_pool.tile(
                     [P, BANK_COLUMNS * PACK], BF16, align_bytes=64, name="grouped"
                 )
                 nc.scalar.copy(
-                    out=grouped[:].bitcast(F32).rearrange("p (s n u) -> p s n u", s=BANK_TILES, u=2),
-                    in_=planes.rearrange("p s u n -> p s n u"),
+                    out=grouped[:].bitcast(F32).rearrange("p (c i u) -> p c u i", i=COLUMN_RUN, u=2),
+                    in_=planes.rearrange("p u (c i) -> p c u i", i=COLUMN_RUN),
                 )
                 staged[index].append((grouped[:], codes[half], scales[half]))
 
         def transpose_last_xh(index, sources, first_word, codes, scales):
             for half in range(OPERAND_BANKS):
                 bank = bank_pool.tile([P, BANK_WORDS], F32, name="bank")
-                planes = bank[:].rearrange("p (s u n) -> p s u n", s=BANK_TILES, u=2)
+                planes = bank[:].rearrange("p (u n) -> p u n", u=2)
                 for s in range(BANK_TILES):
                     words = sources[BANK_TILES * half + s][:].bitcast(F32)
                     for u in range(2):
                         w0 = first_word + u * P
-                        nc.tensor.transpose(planes[:, s, u, :], words[:, w0 : w0 + P], identity[:])
+                        nc.tensor.transpose(planes[:, u, s * P : (s + 1) * P], words[:, w0 : w0 + P], identity[:])
                 columns = slice(half * BANK_COLUMNS * PACK, (half + 1) * BANK_COLUMNS * PACK)
                 nc.scalar.copy(
                     out=last_xh[:HALF, columns]
                     .bitcast(F32)
-                    .rearrange("p (s n u) -> p s n u", s=BANK_TILES, u=2),
-                    in_=planes[:HALF].rearrange("p s u n -> p s n u"),
+                    .rearrange("p (c i u) -> p c u i", i=COLUMN_RUN, u=2),
+                    in_=planes[:HALF].rearrange("p u (c i) -> p c u i", i=COLUMN_RUN),
                 )
             staged[index].append((last_xh[:], codes[:], scales[:]))
 
@@ -299,7 +301,7 @@ def tile_batchedlstm_k_kernel(
                     else:
                         transpose_last_xh(index, sources, first_word, x_codes[g], x_scales[g])
                     if index == 0:
-                        hold_clock()
+                        hold_clock(IDLE_MATMULS)
                 sources = [w_sorted[(h_tile, chunk, gate)] for gate in range(GATES)]
                 codes, scales = [], []
                 for pool in (w_mx_pool, w_late_pool):
@@ -311,7 +313,7 @@ def tile_batchedlstm_k_kernel(
                     index, sources, first_word, [c[:] for c in codes], [c[:] for c in scales]
                 )
                 if index == 0:
-                    hold_clock()
+                    hold_clock(IDLE_MATMULS)
 
         def quantise(index):
             done = sorted_passes[0]
@@ -460,6 +462,7 @@ def tile_batchedlstm_k_kernel(
         for step in range(LOAD_AHEAD):
             load_chunk(step)
         sort_until(sorted_by(0))
+        hold_clock(FIRST_IDLE_MATMULS)
         for index in range(len(rounds) + 1):
             if index == PASSES - 1 + FLIP_LAG:
                 for b in range(BATCH):

@@ -43,7 +43,7 @@ BANK_COLUMNS = BANK_TILES * P
 
 FIRST_IDLE_MATMULS = 4
 IDLE_MATMULS = 3
-SMALL_INPUTS_ROUND = 8
+BIASES_ROUND = 11
 FLIP_LAG = 5
 
 FLOPS = 2 * GATES * HIDDEN * K * N
@@ -82,18 +82,24 @@ def tile_batchedlstm_k_kernel(
         identity = keep.tile([P, P], F32, name="identity")
         make_identity(nc, identity[:])
 
+        warm = keep.tile([P, 1], F32, name="warm")
+        nc.vector.memset(warm[:], 0.0)
+        nc.scalar.activation(out=warm[:], in_=warm[:], func=ACT.Sigmoid)
+
         bias_rows = keep.tile([P, P], BF16, name="bias_rows")
         nc.vector.memset(bias_rows[:], 0.0)
         bias_columns = keep.tile([P, GATES * H_TILES], F32, name="bias_columns")
 
         hidden_raw = keep.tile([P, BATCH, PACK * FRAMES], BF16, name="hidden_raw")
 
-        def load_small_inputs():
+        def load_biases():
             for gate in range(GATES):
                 nc.sync.dma_start(
                     out=bias_rows[gate * H_TILES : (gate + 1) * H_TILES, :],
                     in_=biases[gate].rearrange("(t p) -> t p", p=P),
                 )
+
+        def load_hidden_state():
             nc.sync.dma_start(
                 out=hidden_raw[HALF:, :, :],
                 in_=hidden_state.rearrange("b (p t) f -> p b (t f)", t=PACK),
@@ -101,9 +107,6 @@ def tile_batchedlstm_k_kernel(
 
         last_xh = keep.tile([P, N * PACK], BF16, align_bytes=64, name="last_xh")
 
-        warm = keep.tile([P, 1], F32, name="warm")
-        nc.vector.memset(warm[:], 0.0)
-        nc.scalar.activation(out=warm[:], in_=warm[:], func=ACT.Sigmoid)
 
         bias_rows_f32 = keep.tile([P, P], F32, name="bias_rows_f32")
 
@@ -160,8 +163,10 @@ def tile_batchedlstm_k_kernel(
                         out=w_raw[(h_tile, chunk, gate)][:, piece],
                         in_=weights[gate][h_rows, k0 + piece.start : k0 + piece.stop],
                     )
-            if step == LOAD_AHEAD:
-                load_small_inputs()
+            if step == CHUNKS - 2:
+                load_biases()
+            if step == CHUNKS - 1:
+                load_hidden_state()
             if chunk == CHUNKS - 1:
                 raw = cell_pool.tile([P, BATCH, FRAMES], BF16, name="cell_raw")
                 nc.sync.dma_start(out=raw[:], in_=cell_state.rearrange("b h f -> h b f")[h_rows])
@@ -469,7 +474,7 @@ def tile_batchedlstm_k_kernel(
                     bank = flip_hidden(0, b)
                     nc.scalar.copy(out=flipped[(0, b)][:], in_=bank[:, :FRAMES])
                     store_flipped(0, b, slice(0, 2))
-            if index == SMALL_INPUTS_ROUND + 2:
+            if index == BIASES_ROUND + 2:
                 turn_biases()
             if index < len(rounds):
                 stage(index)
@@ -479,17 +484,19 @@ def tile_batchedlstm_k_kernel(
                 update_cell(0)
             if index < len(rounds):
                 quantise(index)
-            if index == SMALL_INPUTS_ROUND:
+            if index == BIASES_ROUND:
                 widen_biases()
             if index == PASSES - 2:
                 prepare_hidden_state()
             if index == PASSES:
-                for gate in range(GATES):
+                for gate in range(GATES - 1):
                     for b in range(BATCH):
                         activate_gate(0, gate, b)
             if index == PASSES + 1:
                 squash_cell(0)
+            if index == PASSES + 2:
                 for b in range(BATCH):
+                    activate_gate(0, GATES - 1, b)
                     update_hidden(0, b)
                     store_hidden(0, b)
         multiply_late()

from contextlib import ExitStack

import concourse.mybir as mybir
from concourse.masks import make_identity

F32 = mybir.dt.float32
BF16 = mybir.dt.bfloat16
U32 = mybir.dt.uint32
U8 = mybir.dt.uint8
FP8X4 = mybir.dt.float8_e4m3fn_x4
ACT = mybir.ActivationFunctionType
ALU = mybir.AluOpType

P = 128
HALF = P // 2
PACK = 4
K_PASS = P * PACK
BANK_WORDS = 512

BATCH, FRAMES, CHANNELS, HIDDEN = 2, 256, 7936, 256
K = CHANNELS + HIDDEN
PASSES = K // K_PASS
N = BATCH * FRAMES
ROW_TILES = N // P
GATES = 4
H_TILES = HIDDEN // P

CHUNK_PASSES = 2
CHUNK_K = CHUNK_PASSES * K_PASS
COLUMN_RUN = 4
RUN = 8
CHUNKS = K // CHUNK_K
LOAD_AHEAD = 3
HEAD_CHUNKS = 2
SORT_A_STEP = 4 * CHUNK_PASSES
HEAD_STEPS = 2
SORT_LEAD = 14 * CHUNK_PASSES

FREE_BANKS = 4
OPERAND_BANKS = 2
BANK_TILES = 2
BANK_COLUMNS = BANK_TILES * P

FIRST_IDLE_MATMULS = 4
IDLE_MATMULS = 3
BIASES_ROUND = 11
FLIP_LAG = 5

FLOPS = 2 * GATES * HIDDEN * K * N


def tile_batchedlstm_k_kernel(
    tc, x, hidden_state, cell_state, W_f, b_f, W_i, b_i, W_o, b_o, W_g, b_g, out_0, out_1, out_2
):
    nc = tc.nc
    weights = (W_f, W_i, W_g, W_o)
    biases = (b_f, b_i, b_g, b_o)
    gate_functions = (ACT.Sigmoid, ACT.Sigmoid, ACT.Tanh, ACT.Sigmoid)
    x_rows = x.rearrange("b f c -> (b f) c")

    rounds = []
    for h_tile, operands_a_pass in ((0, 2), (1, 1)):
        round_passes = FREE_BANKS // (OPERAND_BANKS * operands_a_pass)
        rounds += [(h_tile, list(range(g, g + round_passes))) for g in range(0, PASSES, round_passes)]

    with ExitStack() as ctx:
        ctx.enter_context(tc.manual_schedule())
        keep = ctx.enter_context(tc.tile_pool(name="keep", bufs=1))
        x_raw_pool = ctx.enter_context(tc.tile_pool(name="x_raw", bufs=ROW_TILES * LOAD_AHEAD))
        w_raw_pool = ctx.enter_context(tc.tile_pool(name="w_raw", bufs=GATES * LOAD_AHEAD))
        x_sorted_pool = ctx.enter_context(tc.tile_pool(name="x_sorted", bufs=3 * ROW_TILES))
        w_sorted_pool = ctx.enter_context(tc.tile_pool(name="w_sorted", bufs=3 * GATES))
        grouped_pool = ctx.enter_context(tc.tile_pool(name="grouped", bufs=2 * FREE_BANKS))
        w_mx_pool = ctx.enter_context(tc.tile_pool(name="w_mx", bufs=4))
        w_late_pool = ctx.enter_context(tc.tile_pool(name="w_late", bufs=PASSES))
        cell_pool = ctx.enter_context(tc.tile_pool(name="cell", bufs=H_TILES * BATCH))
        acc_pool = ctx.enter_context(tc.psum_pool(name="acc", bufs=1))
        bank_pool = ctx.enter_context(tc.psum_pool(name="bank", bufs=FREE_BANKS))

        zeros = keep.tile([P, N], BF16, name="zeros")
        nc.vector.memset(zeros[:], 0.0)
        identity = keep.tile([P, P], F32, name="identity")
        make_identity(nc, identity[:])

        warm = keep.tile([P, 1], F32, name="warm")
        nc.vector.memset(warm[:], 0.0)
        nc.scalar.activation(out=warm[:], in_=warm[:], func=ACT.Sigmoid)

        bias_rows = keep.tile([P, P], BF16, name="bias_rows")
        nc.vector.memset(bias_rows[:], 0.0)
        bias_columns = keep.tile([P, GATES * H_TILES], F32, name="bias_columns")

        hidden_raw = keep.tile([P, BATCH, PACK * FRAMES], BF16, name="hidden_raw")

        def load_biases():
            for gate in range(GATES):
                nc.sync.dma_start(
                    out=bias_rows[gate * H_TILES : (gate + 1) * H_TILES, :],
                    in_=biases[gate].rearrange("(t p) -> t p", p=P),
                )

        def load_hidden_state():
            nc.sync.dma_start(
                out=hidden_raw[HALF:, :, :],
                in_=hidden_state.rearrange("b (p t) f -> p b (t f)", t=PACK),
            )

        last_xh = keep.tile([P, N * PACK], BF16, align_bytes=64, name="last_xh")


        bias_rows_f32 = keep.tile([P, P], F32, name="bias_rows_f32")

        def widen_biases():
            nc.vector.tensor_copy(out=bias_rows_f32[:], in_=bias_rows[:])

        def turn_biases():
            bank = bank_pool.tile([P, BANK_WORDS], F32, name="bank")
            nc.tensor.transpose(bank[:, :P], bias_rows_f32[:], identity[:])
            nc.scalar.copy(out=bias_columns[:], in_=bank[:, : GATES * H_TILES])

        def prepare_hidden_state():
            nc.vector.tensor_copy(
                out=last_xh[HALF:, :].rearrange("p (b f t) -> p b f t", b=BATCH, t=PACK),
                in_=hidden_raw[HALF:, :, :].rearrange("p b (t f) -> p b f t", t=PACK),
            )

        idle_bank = acc_pool.tile([P, N], F32, name="acc0")

        def hold_clock(repeats):
            for repeat in range(repeats):
                nc.tensor.matmul(idle_bank[:], lhsT=zeros[:, :P], rhs=zeros[:], start=True, stop=True)

        x_raw = {}
        w_raw = {}
        cell_raw = {}

        def pieces(step):
            if step < HEAD_CHUNKS or step % CHUNKS == CHUNKS - 1:
                return [(g, g + 1) for g in range(CHUNK_PASSES)]
            return [(0, CHUNK_PASSES)]

        def load_chunk(step):
            h_tile, chunk = divmod(step, CHUNKS)
            h_rows = slice(h_tile * P, (h_tile + 1) * P)
            k0 = chunk * CHUNK_K
            width = min(CHUNK_K, CHANNELS - k0)
            if h_tile == 0:
                for r in range(ROW_TILES):
                    x_raw[(chunk, r)] = x_raw_pool.tile([P, CHUNK_K], BF16, name="x_raw")
            for gate in range(GATES):
                w_raw[(h_tile, chunk, gate)] = w_raw_pool.tile([P, CHUNK_K], BF16, name="w_raw")
            for first, last in pieces(step):
                if h_tile == 0:
                    piece = slice(first * K_PASS, min(last * K_PASS, width))
                    for r in range(ROW_TILES):
                        nc.sync.dma_start(
                            out=x_raw[(chunk, r)][:, piece],
                            in_=x_rows[r * P : (r + 1) * P, k0 + piece.start : k0 + piece.stop],
                        )
                piece = slice(first * K_PASS, last * K_PASS)
                for gate in range(GATES):
                    nc.sync.dma_start(
                        out=w_raw[(h_tile, chunk, gate)][:, piece],
                        in_=weights[gate][h_rows, k0 + piece.start : k0 + piece.stop],
                    )
            if step == CHUNKS - 2:
                load_biases()
            if step == CHUNKS - 1:
                load_hidden_state()
            if chunk == CHUNKS - 1:
                raw = cell_pool.tile([P, BATCH, FRAMES], BF16, name="cell_raw")
                nc.sync.dma_start(out=raw[:], in_=cell_state.rearrange("b h f -> h b f")[h_rows])
                cell_raw[h_tile] = raw

        x_sorted = {}
        w_sorted = {}
        to_sort = []
        for step in range(H_TILES * CHUNKS):
            for first, last in pieces(step):
                if step < CHUNKS:
                    to_sort += [(step, "x", r, first, last) for r in range(ROW_TILES)]
                to_sort += [(step, "w", gate, first, last) for gate in range(GATES)]
        sorted_passes = [0]

        def sort_tile():
            step, operand, tile, first, last = to_sort.pop(0)
            sorted_passes[0] += last - first
            h_tile, chunk = divmod(step, CHUNKS)
            if operand == "x":
                raw = x_raw[(chunk, tile)]
                if first == 0:
                    x_sorted[(chunk, tile)] = x_sorted_pool.tile([P, CHUNK_K], BF16, name="x_sorted")
                planes = x_sorted[(chunk, tile)]
            else:
                raw = w_raw[(h_tile, chunk, tile)]
                if first == 0:
                    w_sorted[(h_tile, chunk, tile)] = w_sorted_pool.tile(
                        [P, CHUNK_K], BF16, name="w_sorted"
                    )
                planes = w_sorted[(h_tile, chunk, tile)]
            by_plane = planes[:].bitcast(F32).rearrange("p (m u w) -> p m u w", u=2, w=P)
            k0 = chunk * CHUNK_K + first * K_PASS
            width = (last - first) * K_PASS
            if operand == "x":
                width = min(width, CHANNELS - k0)
            words = raw[:, first * K_PASS : first * K_PASS + width].bitcast(F32)
            if last - first == CHUNK_PASSES:
                nc.vector.tensor_copy(
                    out=by_plane.rearrange("p m u (q i) -> p m u q i", i=RUN),
                    in_=words.rearrange("p (m q u i) -> p m u q i", m=CHUNK_PASSES, u=2, i=RUN),
                )
            else:
                run = RUN if k0 < K - K_PASS else 1
                n = width // PACK
                if n < P:
                    nc.gpsimd.memset(by_plane[:, first, :, n:], 0.0)
                nc.vector.tensor_copy(
                    out=by_plane[:, first, :, :n].rearrange("p u (h q i) -> p h u q i", h=2, i=run),
                    in_=words.rearrange("p (h q u i) -> p h u q i", h=2, u=2, i=run),
                )
            if len(to_sort) == 0 or to_sort[0][0] != step:
                if step + LOAD_AHEAD < H_TILES * CHUNKS:
                    load_chunk(step + LOAD_AHEAD)

        def sort_until(count):
            while sorted_passes[0] < count and len(to_sort) > 0:
                sort_tile()

        def sorted_by(round_index):
            if round_index < PASSES:
                return (ROW_TILES + GATES) * (round_index + 1)
            h_passes = CHUNK_PASSES * (round_index - PASSES + 1)
            return (ROW_TILES + GATES) * PASSES + GATES * h_passes

        def sort_target(index):
            if index < HEAD_STEPS:
                return sorted_by(index + 1)
            target = SORT_LEAD + SORT_A_STEP * index
            return target if index + 2 < PASSES else min(target, sorted_by(index + 2))

        staged = {}

        def transpose_operand(index, sources, first_word, codes, scales):
            for half in range(OPERAND_BANKS):
                bank = bank_pool.tile([P, BANK_WORDS], F32, name="bank")
                planes = bank[:].rearrange("p (u n) -> p u n", u=2)
                for s in range(BANK_TILES):
                    words = sources[BANK_TILES * half + s][:].bitcast(F32)
                    for u in range(2):
                        w0 = first_word + u * P
                        nc.tensor.transpose(planes[:, u, s * P : (s + 1) * P], words[:, w0 : w0 + P], identity[:])
                grouped = grouped_pool.tile(
                    [P, BANK_COLUMNS * PACK], BF16, align_bytes=64, name="grouped"
                )
                nc.scalar.copy(
                    out=grouped[:].bitcast(F32).rearrange("p (c i u) -> p c u i", i=COLUMN_RUN, u=2),
                    in_=planes.rearrange("p u (c i) -> p c u i", i=COLUMN_RUN),
                )
                staged[index].append((grouped[:], codes[half], scales[half]))

        def transpose_last_xh(index, sources, first_word, codes, scales):
            for half in range(OPERAND_BANKS):
                bank = bank_pool.tile([P, BANK_WORDS], F32, name="bank")
                planes = bank[:].rearrange("p (u n) -> p u n", u=2)
                for s in range(BANK_TILES):
                    words = sources[BANK_TILES * half + s][:].bitcast(F32)
                    for u in range(2):
                        w0 = first_word + u * P
                        nc.tensor.transpose(planes[:, u, s * P : (s + 1) * P], words[:, w0 : w0 + P], identity[:])
                columns = slice(half * BANK_COLUMNS * PACK, (half + 1) * BANK_COLUMNS * PACK)
                nc.scalar.copy(
                    out=last_xh[:HALF, columns]
                    .bitcast(F32)
                    .rearrange("p (c i u) -> p c u i", i=COLUMN_RUN, u=2),
                    in_=planes[:HALF].rearrange("p u (c i) -> p c u i", i=COLUMN_RUN),
                )
            staged[index].append((last_xh[:], codes[:], scales[:]))

        x_codes = {}
        x_scales = {}
        w_codes = {}
        w_scales = {}

        def stage(index):
            h_tile, passes = rounds[index]
            staged[index] = []
            for g in passes:
                chunk, pass_in_chunk = divmod(g, CHUNK_PASSES)
                first_word = pass_in_chunk * 2 * P
                if h_tile == 0:
                    sources = [x_sorted[(chunk, r)] for r in range(ROW_TILES)]
                    x_codes[g] = keep.tile([P, N], U32, align_bytes=64, name="x_codes%d" % g)
                    x_scales[g] = keep.tile([P, N], U8, align_bytes=64, name="x_scales%d" % g)
                    if g < PASSES - 1:
                        columns = [
                            slice(half * BANK_COLUMNS, (half + 1) * BANK_COLUMNS)
                            for half in range(OPERAND_BANKS)
                        ]
                        transpose_operand(
                            index,
                            sources,
                            first_word,
                            [x_codes[g][:, c] for c in columns],
                            [x_scales[g][:, c] for c in columns],
                        )
                    else:
                        transpose_last_xh(index, sources, first_word, x_codes[g], x_scales[g])
                    if index == 0:
                        hold_clock(IDLE_MATMULS)
                sources = [w_sorted[(h_tile, chunk, gate)] for gate in range(GATES)]
                codes, scales = [], []
                for pool in (w_mx_pool, w_late_pool):
                    codes.append(pool.tile([P, BANK_COLUMNS], U32, align_bytes=64, name="w_codes"))
                    scales.append(pool.tile([P, BANK_COLUMNS], U8, align_bytes=64, name="w_scales"))
                w_codes[(h_tile, g)] = codes
                w_scales[(h_tile, g)] = scales
                transpose_operand(
                    index, sources, first_word, [c[:] for c in codes], [c[:] for c in scales]
                )
                if index == 0:
                    hold_clock(IDLE_MATMULS)

        def quantise(index):
            done = sorted_passes[0]
            missing = max(0, sort_target(index) - done)
            for position, (grouped, codes, scales) in enumerate(staged[index]):
                nc.vector.quantize_mx(out=codes.bitcast(FP8X4), scales=scales, in_=grouped)
                sort_until(done + missing * (position + 1) // len(staged[index]))

        acc = {}

        def gate_pass(out, h_tile, gate, g, columns):
            half, gate_in_half = divmod(gate, BANK_TILES)
            rows = slice(gate_in_half * P, (gate_in_half + 1) * P)
            nc.tensor.matmul_mx(
                out=out,
                lhsT=w_codes[(h_tile, g)][half][:, rows].bitcast(FP8X4),
                lhsT_scale=w_scales[(h_tile, g)][half][:, rows],
                rhs=x_codes[g][:, columns].bitcast(FP8X4),
                rhs_scale=x_scales[g][:, columns],
                start=(g == 0),
                stop=(g == PASSES - 1),
            )

        banks = {}

        def multiply(index):
            h_tile, passes = rounds[index]
            for gate in range(GATES if h_tile < H_TILES - 1 else GATES - 1):
                if passes[0] == 0:
                    banks[gate] = acc_pool.tile([P, N], F32, name="acc%d" % gate)
                    for b in range(BATCH):
                        acc[(h_tile, gate, b)] = banks[gate][:, b * FRAMES : (b + 1) * FRAMES]
                for g in passes:
                    gate_pass(banks[gate][:], h_tile, gate, g, slice(0, N))

        def multiply_late():
            h_tile, gate = H_TILES - 1, GATES - 1
            for b in range(BATCH):
                bank = bank_pool.tile([P, BANK_WORDS], F32, name="bank")
                acc[(h_tile, gate, b)] = bank[:, :FRAMES]
                for g in range(PASSES):
                    gate_pass(bank[:, :FRAMES], h_tile, gate, g, slice(b * FRAMES, (b + 1) * FRAMES))

        activated = {}
        new_cell = {}
        squashed = {}
        new_hidden = {}
        flipped = {}

        def cell_tile(name):
            return cell_pool.tile([P, FRAMES], F32, name=name)

        def activate_gate(h_tile, gate, b, columns=slice(0, FRAMES)):
            if columns.start == 0:
                activated[(h_tile, gate, b)] = cell_tile("gate%d" % gate)
            bias_column = gate * H_TILES + h_tile
            nc.scalar.activation(
                out=activated[(h_tile, gate, b)][:, columns],
                in_=acc[(h_tile, gate, b)][:, columns],
                func=gate_functions[gate],
                bias=bias_columns[:, bias_column : bias_column + 1],
                scale=1.0,
            )

        def update_cell(h_tile):
            h_rows = slice(h_tile * P, (h_tile + 1) * P)
            kept = {}
            for b in range(BATCH):
                kept[b] = cell_tile("kept")
                nc.vector.tensor_tensor(
                    out=kept[b][:],
                    in0=activated[(h_tile, 0, b)][:],
                    in1=cell_raw[h_tile][:, b, :],
                    op=ALU.mult,
                )
            for b in range(BATCH):
                added = cell_tile("added")
                nc.vector.tensor_tensor(
                    out=added[:],
                    in0=activated[(h_tile, 1, b)][:],
                    in1=activated[(h_tile, 2, b)][:],
                    op=ALU.mult,
                )
                new_cell[(h_tile, b)] = cell_tile("new_cell")
                nc.vector.tensor_tensor(
                    out=new_cell[(h_tile, b)][:], in0=kept[b][:], in1=added[:], op=ALU.add
                )
                nc.sync.dma_start(out=out_2[b, h_rows, :], in_=new_cell[(h_tile, b)][:])

        def squash_cell(h_tile):
            for b in range(BATCH):
                squashed[(h_tile, b)] = cell_tile("squashed")
                nc.scalar.activation(
                    out=squashed[(h_tile, b)][:], in_=new_cell[(h_tile, b)][:], func=ACT.Tanh
                )

        def update_hidden(h_tile, b, columns=slice(0, FRAMES)):
            if columns.start == 0:
                new_hidden[(h_tile, b)] = cell_tile("new_hidden")
            nc.vector.tensor_tensor(
                out=new_hidden[(h_tile, b)][:, columns],
                in0=squashed[(h_tile, b)][:, columns],
                in1=activated[(h_tile, GATES - 1, b)][:, columns],
                op=ALU.mult,
            )

        def store_hidden(h_tile, b):
            h_rows = slice(h_tile * P, (h_tile + 1) * P)
            nc.sync.dma_start(out=out_1[b, h_rows, :], in_=new_hidden[(h_tile, b)][:])

        def flip_hidden(h_tile, b):
            bank = bank_pool.tile([P, BANK_WORDS], F32, name="bank")
            for columns in f_tiles:
                nc.tensor.transpose(bank[:, columns], new_hidden[(h_tile, b)][:, columns], identity[:])
            flipped[(h_tile, b)] = cell_tile("flipped")
            return bank

        def store_flipped(h_tile, b, tiles):
            h_columns = slice(h_tile * P, (h_tile + 1) * P)
            nc.sync.dma_start(
                out=out_0[b].rearrange("(t p) h -> p t h", p=P)[:, tiles, h_columns],
                in_=flipped[(h_tile, b)][:].rearrange("p (t h) -> p t h", h=P)[:, tiles, :],
            )

        f_tiles = [slice(t * P, (t + 1) * P) for t in range(FRAMES // P)]

        def finish_last_tile():
            h_tile = H_TILES - 1
            for gate in range(GATES - 1):
                for b in range(BATCH):
                    activate_gate(h_tile, gate, b)
            update_cell(h_tile)
            squash_cell(h_tile)
            for b in range(BATCH):
                for columns in f_tiles:
                    activate_gate(h_tile, GATES - 1, b, columns)
                    update_hidden(h_tile, b, columns)
                store_hidden(h_tile, b)
            turned = [flip_hidden(h_tile, b) for b in range(BATCH)]
            nc.scalar.copy(out=flipped[(h_tile, 0)][:], in_=turned[0][:, :FRAMES])
            store_flipped(h_tile, 0, slice(0, 2))
            for t, columns in enumerate(f_tiles):
                nc.vector.tensor_copy(out=flipped[(h_tile, 1)][:, columns], in_=turned[1][:, columns])
                store_flipped(h_tile, 1, slice(t, t + 1))

        for step in range(LOAD_AHEAD):
            load_chunk(step)
        sort_until(sorted_by(0))
        hold_clock(FIRST_IDLE_MATMULS)
        for index in range(len(rounds) + 1):
            if index == PASSES - 1 + FLIP_LAG:
                for b in range(BATCH):
                    bank = flip_hidden(0, b)
                    nc.scalar.copy(out=flipped[(0, b)][:], in_=bank[:, :FRAMES])
                    store_flipped(0, b, slice(0, 2))
            if index == BIASES_ROUND + 2:
                turn_biases()
            if index < len(rounds):
                stage(index)
            if index > 0:
                multiply(index - 1)
            if index == PASSES + 1:
                update_cell(0)
            if index < len(rounds):
                quantise(index)
            if index == BIASES_ROUND:
                widen_biases()
            if index == PASSES - 2:
                prepare_hidden_state()
            if index == PASSES:
                for gate in range(GATES - 1):
                    for b in range(BATCH):
                        activate_gate(0, gate, b)
            if index == PASSES + 1:
                squash_cell(0)
            if index == PASSES + 2:
                for b in range(BATCH):
                    activate_gate(0, GATES - 1, b)
                    update_hidden(0, b)
                    store_hidden(0, b)
        multiply_late()
        finish_last_tile()
